import numpy as np
import ml_dtypes


def mxq(x, axis, fmt="e4m3"):
    dtype, down = {"e4m3": (ml_dtypes.float8_e4m3fn, 7), "e5m2": (ml_dtypes.float8_e5m2, 14)}[fmt]
    v = np.moveaxis(np.asarray(x, np.float32).astype(ml_dtypes.bfloat16).astype(np.float64), axis, -1)
    blocks = v.reshape(v.shape[:-1] + (-1, 32))
    amax = np.abs(blocks).max(-1, keepdims=True)
    byte = np.maximum(np.where(amax > 0, np.frexp(amax)[1] - 1 + 127, 0) - down, 1)
    scale = np.exp2(byte - 127.0)
    codes = (blocks / scale).astype(np.float32).astype(dtype).astype(np.float64)
    return np.moveaxis((codes * scale).reshape(v.shape), -1, axis)


WIDE = False


def mx_kscale(k):
    if not WIDE:
        return np.ones(k)
    levels = np.array([10, -10, 5, -5, 0])
    a = np.random.permutation(np.resize(levels, k // 512 * 4)).reshape(k // 512, 4)
    idx = np.arange(k)
    return np.exp2(a[idx // 512, idx % 128 // 32])


BF16 = ml_dtypes.bfloat16


def bf(x):
    return np.asarray(x, np.float32).astype(BF16)


def f64(x):
    return np.asarray(x).astype(np.float64)


B, C_IN, N, L, C_OUT, ORDER, EMBED, SUP_LEN = 4, 32, 1024, 12, 64, 3, 10, 2


def setup_inputs():
    s = mx_kscale(N)
    return {"a": bf(np.random.standard_normal((N, N)) / np.sqrt(N) * s[None, :] / s[:, None]),
            "x": bf(np.random.standard_normal((B, C_IN, N, L)) / s[None, None, :, None])}


def reference(a, x):
    a, x = f64(a), f64(x)
    a_left = mxq(a, 1, "e4m3")
    xq = mxq(x, 2, "e4m3")
    t2 = 2.0 * (a_left @ mxq(a, 0, "e4m3")) - np.eye(N)
    y1 = a_left @ xq
    y2 = mxq(t2, 1, "e4m3") @ xq
    return np.stack([y1, y2], axis=1).transpose(0, 1, 3, 2, 4)

@@ -1,0 +1,202 @@
+from contextlib import ExitStack
+
+import concourse.mybir as mybir
+from concourse.masks import make_identity
+
+F32 = mybir.dt.float32
+BF16 = mybir.dt.bfloat16
+U32 = mybir.dt.uint32
+U8 = mybir.dt.uint8
+FP8X4 = mybir.dt.float8_e4m3fn_x4
+ALU = mybir.AluOpType
+ACT = mybir.ActivationFunctionType
+
+P = 128
+FLOPS = 2 * 1024 * 1024 * (1024 + 1536 + 1536)
+MANUAL = False
+
+Y1_ENG = ["s", "s", "v", "s", "s", "v", "s", "s"]
+Y2_ENG = ["v", "s", "s", "v", "s", "s", "v", "s"]
+
+
+def tile_gcn_pa_kernel(tc, a, x, out):
+    nc = tc.nc
+    with ExitStack() as ctx:
+        if MANUAL:
+            ctx.enter_context(tc.manual_schedule())
+        keep = ctx.enter_context(tc.tile_pool(name="keep", bufs=1))
+        resp = ctx.enter_context(tc.tile_pool(name="resp", bufs=6))
+        psum = ctx.enter_context(tc.psum_pool(name="psum", bufs=8))
+
+        def copy(eng, dst, src):
+            if eng == "v":
+                nc.vector.tensor_copy(out=dst, in_=src)
+            else:
+                nc.scalar.copy(out=dst, in_=src)
+
+        wide = keep.tile([P, 7 * P], F32, name="wide")
+        nc.gpsimd.memset(wide[:], 0.0)
+        make_identity(nc, wide[:, 3 * P : 4 * P], nomemset=True)
+        ident = wide[:, 3 * P : 4 * P]
+
+        x_sb = keep.tile([P, 12288], BF16, name="x_sb")
+        a_sb = keep.tile([P, 8192], BF16, name="a_sb")
+        xv = x.rearrange("b c m l -> (b c) (m l)")
+        for q in range(4):
+            nc.sync.dma_start(out=x_sb[:, 3072 * q : 3072 * (q + 1)], in_=xv[:, 3072 * q : 3072 * (q + 1)])
+        for q in range(4):
+            nc.sync.dma_start(
+                out=a_sb[:, 2048 * q : 2048 * (q + 1)],
+                in_=a[256 * q : 256 * (q + 1), :].rearrange("(p e) m -> p (e m)", e=2),
+            )
+
+        x_words = x_sb[:].bitcast(F32).rearrange("b (q p e h) -> b q e h p", q=4, p=P, e=2, h=6)
+        a32 = a_sb[:].bitcast(F32)
+
+        xg = keep.tile([P, 12288], BF16, name="xg", align_bytes=64)
+        xc = keep.tile([P, 3072], U32, name="xc", align_bytes=64)
+        xs = keep.tile([P, 3072], U8, name="xs", align_bytes=64)
+        alg = keep.tile([P, 8192], BF16, name="alg", align_bytes=64)
+        alc = keep.tile([P, 2048], U32, name="alc", align_bytes=64)
+        als = keep.tile([P, 2048], U8, name="als", align_bytes=64)
+        arg = keep.tile([P, 8192], BF16, name="arg", align_bytes=64)
+        arc = keep.tile([P, 2048], U32, name="arc", align_bytes=64)
+        ars = keep.tile([P, 2048], U8, name="ars", align_bytes=64)
+        t2g = keep.tile([P, 8192], BF16, name="t2g", align_bytes=64)
+        t2c = keep.tile([P, 2048], U32, name="t2c", align_bytes=64)
+        t2s = keep.tile([P, 2048], U8, name="t2s", align_bytes=64)
+        alg32 = alg[:].bitcast(F32)
+
+        def quant(codes, scales, grouped, w0, w):
+            nc.vector.quantize_mx(
+                out=codes[:, w0 : w0 + w].bitcast(FP8X4),
+                scales=scales[:, w0 : w0 + w],
+                in_=grouped[:, 4 * w0 : 4 * (w0 + w)],
+            )
+
+        def mx(dst, lc, ls, l0, rc, rs, r0, n, start, stop):
+            nc.tensor.matmul_mx(
+                out=dst,
+                lhsT=lc[:, l0 : l0 + P].bitcast(FP8X4),
+                lhsT_scale=ls[:, l0 : l0 + P],
+                rhs=rc[:, r0 : r0 + n].bitcast(FP8X4),
+                rhs_scale=rs[:, r0 : r0 + n],
+                start=start,
+                stop=stop,
+            )
+
+        def xt(g, h, eng):
+            bank = psum.tile([P, 512], F32, name="bank", tag="bank")
+            for u in range(2):
+                for e in range(2):
+                    t = 2 * u + e
+                    nc.tensor.transpose(bank[:, t * P : (t + 1) * P], x_words[:, 2 * g + u, e, h, :], ident)
+            o = (g * 6 + h) * 1024
+            copy(
+                eng,
+                xg[:, o : o + 1024].rearrange("p (b k t) -> p b k t", k=2, t=4),
+                bank[:].bitcast(BF16).rearrange("p (t b k) -> p b k t", t=4, k=2),
+            )
+
+        def at(tau, eng):
+            bank = psum.tile([P, 512], F32, name="bank", tag="bank")
+            for i in range(4):
+                nc.tensor.transpose(bank[:, i * P : (i + 1) * P], a32[:, tau * 512 + i * P : tau * 512 + (i + 1) * P], ident)
+            copy(
+                eng,
+                alg32[:, tau * 512 : (tau + 1) * 512].rearrange("p (g n u) -> p g n u", g=2, u=2),
+                bank[:].rearrange("p (g u n) -> p g n u", g=2, u=2),
+            )
+
+        a_rows = a_sb[:].rearrange("p (g j q n e) -> p g q e n j", g=2, j=4, q=4, n=P, e=2)
+
+        def ar(g, q):
+            o = g * 4096 + q * 1024
+            nc.vector.tensor_copy(
+                out=arg[:, o : o + 1024].rearrange("p (e n j) -> p e n j", e=2, j=4),
+                in_=a_rows[:, g, q],
+            )
+
+        res_tiles = {}
+
+        def ypass(term, tau, c, lc, ls, eng):
+            bank = psum.tile([P, 512], F32, name="bank", tag="bank")
+            for g in range(2):
+                mx(bank[:], lc, ls, tau * 256 + g * P, xc, xs, g * 1536 + c * 512, 512, g == 0, g == 1)
+            if c == 0:
+                res = resp.tile([P, 1536], F32, name="res", tag="res")
+                res_tiles[(term, tau)] = res
+            res = res_tiles[(term, tau)]
+            copy(
+                eng,
+                res[:].rearrange("p (b l) -> p b l", l=12)[:, :, 4 * c : 4 * c + 4].rearrange("p b (h k) -> p b h k", k=2),
+                bank[:].rearrange("p (h b k) -> p b h k", h=2, k=2),
+            )
+            if c == 2:
+                dst = out[:, term].rearrange("b (q p e) c l -> q e p b (c l)", q=4, p=P, e=2)[tau // 2, tau % 2]
+                nc.sync.dma_start(out=dst, in_=res[:].rearrange("p (b f) -> p b f", b=4))
+
+        def ua(j):
+            for gp in range(2):
+                bank = psum.tile([P, 512], F32, name="bank", tag="bank")
+                for tp in range(4):
+                    for g in range(2):
+                        mx(bank[:, tp * P : (tp + 1) * P], arc, ars, g * 1024 + (4 * gp + tp) * P,
+                           alc, als, j * 256 + g * P, P, g == 0, g == 1)
+                o = j * 1024 + gp * 512
+                dst = t2g[:, o : o + 512].rearrange("p (n t) -> p n t", t=4)
+                src = bank[:].rearrange("p (t n) -> p n t", t=4)
+                if j // 4 == gp:
+                    w0 = (3 - j % 4) * P
+                    nc.vector.scalar_tensor_tensor(
+                        out=dst, in0=src, scalar=2.0,
+                        in1=wide[:, w0 : w0 + 512].rearrange("p (t n) -> p n t", t=4),
+                        op0=ALU.mult, op1=ALU.subtract,
+                    )
+                else:
+                    nc.scalar.activation(out=dst, in_=src, func=ACT.Copy, scale=2.0)
+
+        for h in range(6):
+            xt(0, h, "v" if h % 2 == 0 else "s")
+        xt(1, 0, "s")
+        xt(1, 1, "v")
+        quant(xc, xs, xg, 0, 512)
+        at(0, "s")
+        at(1, "s")
+        quant(xc, xs, xg, 1536, 512)
+        xt(1, 2, "s")
+        xt(1, 3, "v")
+        quant(alc, als, alg, 0, 512)
+        at(2, "s")
+        at(3, "s")
+        quant(xc, xs, xg, 512, 512)
+        xt(1, 4, "s")
+        xt(1, 5, "v")
+        quant(alc, als, alg, 512, 512)
+        quant(xc, xs, xg, 1536 + 512, 512)
+        quant(xc, xs, xg, 1024, 512)
+        quant(xc, xs, xg, 1536 + 1024, 512)
+        for tau in range(4):
+            ypass(0, tau, 0, alc, als, Y1_ENG[tau])
+        for tau in range(4, 8):
+            at(tau, "s")
+        for c in range(1, 3):
+            for tau in range(4):
+                ypass(0, tau, c, alc, als, Y1_ENG[tau])
+        quant(alc, als, alg, 1024, 512)
+        quant(alc, als, alg, 1536, 512)
+        for g in range(2):
+            for q in range(4):
+                ar(g, q)
+        for tau in range(4, 8):
+            for c in range(3):
+                ypass(0, tau, c, alc, als, Y1_ENG[tau])
+        quant(arc, ars, arg, 0, 1024)
+        quant(arc, ars, arg, 1024, 1024)
+        for j in range(10):
+            if j < 8:
+                ua(j)
+                quant(t2c, t2s, t2g, j * 256, 256)
+            if j >= 2:
+                for c in range(3):
+                    ypass(1, j - 2, c, t2c, t2s, Y2_ENG[j - 2])

@@ -13,10 +13,10 @@ ACT = mybir.ActivationFunctionType
 
 P = 128
 FLOPS = 2 * 1024 * 1024 * (1024 + 1536 + 1536)
-MANUAL = False
+MANUAL = True
 
-Y1_ENG = ["s", "s", "v", "s", "s", "v", "s", "s"]
-Y2_ENG = ["v", "s", "s", "v", "s", "s", "v", "s"]
+Y1_ENG = ["s", "s", "s", "s", "s", "s", "s", "v"]
+Y2_ENG = ["s", "v", "s", "s", "v", "s", "s", "v"]
 
 
 def tile_gcn_pa_kernel(tc, a, x, out):
@@ -25,7 +25,7 @@ def tile_gcn_pa_kernel(tc, a, x, out):
         if MANUAL:
             ctx.enter_context(tc.manual_schedule())
         keep = ctx.enter_context(tc.tile_pool(name="keep", bufs=1))
-        resp = ctx.enter_context(tc.tile_pool(name="resp", bufs=6))
+        resp = ctx.enter_context(tc.tile_pool(name="resp", bufs=8))
         psum = ctx.enter_context(tc.psum_pool(name="psum", bufs=8))
 
         def copy(eng, dst, src):
@@ -85,17 +85,22 @@ def tile_gcn_pa_kernel(tc, a, x, out):
                 stop=stop,
             )
 
-        def xt(g, h, eng):
-            bank = psum.tile([P, 512], F32, name="bank", tag="bank")
-            for u in range(2):
+        banks = {}
+
+        def xt(g, u):
+            for h in range(6):
+                if u == 0:
+                    banks[("x", g, h)] = psum.tile([P, 512], F32, name="bank", tag="bank")
                 for e in range(2):
                     t = 2 * u + e
-                    nc.tensor.transpose(bank[:, t * P : (t + 1) * P], x_words[:, 2 * g + u, e, h, :], ident)
+                    nc.tensor.transpose(banks[("x", g, h)][:, t * P : (t + 1) * P], x_words[:, 2 * g + u, e, h, :], ident)
+
+        def xe(g, h, eng):
             o = (g * 6 + h) * 1024
             copy(
                 eng,
                 xg[:, o : o + 1024].rearrange("p (b k t) -> p b k t", k=2, t=4),
-                bank[:].bitcast(BF16).rearrange("p (t b k) -> p b k t", t=4, k=2),
+                banks[("x", g, h)][:].bitcast(BF16).rearrange("p (t b k) -> p b k t", t=4, k=2),
             )
 
         def at(tau, eng):
@@ -156,47 +161,58 @@ def tile_gcn_pa_kernel(tc, a, x, out):
                 else:
                     nc.scalar.activation(out=dst, in_=src, func=ACT.Copy, scale=2.0)
 
+        def xq(g, c):
+            quant(xc, xs, xg, g * 1536 + c * 512, 512)
+
+        def aq(pair):
+            quant(alc, als, alg, pair * 512, 512)
+
+        xt(0, 0)
+        xt(0, 1)
         for h in range(6):
-            xt(0, h, "v" if h % 2 == 0 else "s")
-        xt(1, 0, "s")
-        xt(1, 1, "v")
-        quant(xc, xs, xg, 0, 512)
+            xe(0, h, "v" if h % 2 == 0 else "s")
+        xt(1, 0)
+        xt(1, 1)
+        xe(1, 0, "s")
+        xe(1, 1, "v")
+        xq(0, 0)
         at(0, "s")
         at(1, "s")
-        quant(xc, xs, xg, 1536, 512)
-        xt(1, 2, "s")
-        xt(1, 3, "v")
-        quant(alc, als, alg, 0, 512)
+        xq(1, 0)
+        aq(0)
+        xe(1, 2, "s")
+        xe(1, 3, "v")
         at(2, "s")
         at(3, "s")
-        quant(xc, xs, xg, 512, 512)
-        xt(1, 4, "s")
-        xt(1, 5, "v")
-        quant(alc, als, alg, 512, 512)
-        quant(xc, xs, xg, 1536 + 512, 512)
-        quant(xc, xs, xg, 1024, 512)
-        quant(xc, xs, xg, 1536 + 1024, 512)
+        xq(0, 1)
+        aq(1)
+        xe(1, 4, "s")
+        xq(1, 1)
+        xe(1, 5, "v")
+        xq(0, 2)
+        xq(1, 2)
         for tau in range(4):
             ypass(0, tau, 0, alc, als, Y1_ENG[tau])
+        for q in range(4):
+            ar(0, q)
         for tau in range(4, 8):
             at(tau, "s")
+        aq(2)
+        aq(3)
         for c in range(1, 3):
             for tau in range(4):
                 ypass(0, tau, c, alc, als, Y1_ENG[tau])
-        quant(alc, als, alg, 1024, 512)
-        quant(alc, als, alg, 1536, 512)
-        for g in range(2):
-            for q in range(4):
-                ar(g, q)
+        for q in range(4):
+            ar(1, q)
+        quant(arc, ars, arg, 0, 1024)
+        quant(arc, ars, arg, 1024, 1024)
         for tau in range(4, 8):
             for c in range(3):
                 ypass(0, tau, c, alc, als, Y1_ENG[tau])
-        quant(arc, ars, arg, 0, 1024)
-        quant(arc, ars, arg, 1024, 1024)
-        for j in range(10):
+        for j in range(9):
             if j < 8:
                 ua(j)
                 quant(t2c, t2s, t2g, j * 256, 256)
-            if j >= 2:
+            if j >= 1:
                 for c in range(3):
-                    ypass(1, j - 2, c, t2c, t2s, Y2_ENG[j - 2])
+                    ypass(1, j - 1, c, t2c, t2s, Y2_ENG[j - 1])

@@ -12,207 +12,215 @@ ALU = mybir.AluOpType
 ACT = mybir.ActivationFunctionType
 
 P = 128
-FLOPS = 2 * 1024 * 1024 * (1024 + 1536 + 1536)
-MANUAL = True
-
-Y1_ENG = ["s", "s", "s", "s", "s", "s", "s", "v"]
-Y2_ENG = ["s", "v", "s", "s", "v", "s", "s", "v"]
+TILES = 8
+PASSES = 2
+SLOTS = 4
+NODES = 1024
+STEP_PAIRS = 6
+COLS = 1536
+CHUNK = 512
+CHUNKS = COLS // CHUNK
+ROW_WORDS = NODES // 2
+FLOPS = 2 * NODES * NODES * (NODES + 2 * COLS)
 
 
 def tile_gcn_pa_kernel(tc, a, x, out):
     nc = tc.nc
     with ExitStack() as ctx:
-        if MANUAL:
-            ctx.enter_context(tc.manual_schedule())
+        ctx.enter_context(tc.manual_schedule())
         keep = ctx.enter_context(tc.tile_pool(name="keep", bufs=1))
-        resp = ctx.enter_context(tc.tile_pool(name="resp", bufs=8))
+        results = ctx.enter_context(tc.tile_pool(name="results", bufs=8))
         psum = ctx.enter_context(tc.psum_pool(name="psum", bufs=8))
 
-        def copy(eng, dst, src):
-            if eng == "v":
+        def new_bank():
+            bank = psum.tile([P, CHUNK], F32, name="bank", tag="bank")
+            return bank
+
+        def copy(engine, dst, src):
+            if engine == "vector":
                 nc.vector.tensor_copy(out=dst, in_=src)
             else:
                 nc.scalar.copy(out=dst, in_=src)
 
-        wide = keep.tile([P, 7 * P], F32, name="wide")
-        nc.gpsimd.memset(wide[:], 0.0)
-        make_identity(nc, wide[:, 3 * P : 4 * P], nomemset=True)
-        ident = wide[:, 3 * P : 4 * P]
+        def quantise(codes, scales, grouped, first, width):
+            nc.vector.quantize_mx(
+                out=codes[:, first : first + width].bitcast(FP8X4),
+                scales=scales[:, first : first + width],
+                in_=grouped[:, SLOTS * first : SLOTS * (first + width)],
+            )
 
-        x_sb = keep.tile([P, 12288], BF16, name="x_sb")
-        a_sb = keep.tile([P, 8192], BF16, name="a_sb")
-        xv = x.rearrange("b c m l -> (b c) (m l)")
+        def mx_pass(acc, left, left_first, right, right_first, width, g):
+            nc.tensor.matmul_mx(
+                out=acc,
+                lhsT=left[0][:, left_first : left_first + P].bitcast(FP8X4),
+                lhsT_scale=left[1][:, left_first : left_first + P],
+                rhs=right[0][:, right_first : right_first + width].bitcast(FP8X4),
+                rhs_scale=right[1][:, right_first : right_first + width],
+                start=(g == 0),
+                stop=(g == PASSES - 1),
+            )
+
+        eye_strip = keep.tile([P, 7 * P], F32, name="eye_strip")
+        nc.gpsimd.memset(eye_strip[:], 0.0)
+        make_identity(nc, eye_strip[:, 3 * P : 4 * P], nomemset=True)
+        identity = eye_strip[:, 3 * P : 4 * P]
+
+        x_rows = keep.tile([P, NODES * 12], BF16, name="x_rows")
+        a_rows = keep.tile([P, TILES * NODES], BF16, name="a_rows")
+        x_flat = x.rearrange("b c m l -> (b c) (m l)")
         for q in range(4):
-            nc.sync.dma_start(out=x_sb[:, 3072 * q : 3072 * (q + 1)], in_=xv[:, 3072 * q : 3072 * (q + 1)])
+            piece = slice(3072 * q, 3072 * (q + 1))
+            nc.sync.dma_start(out=x_rows[:, piece], in_=x_flat[:, piece])
         for q in range(4):
             nc.sync.dma_start(
-                out=a_sb[:, 2048 * q : 2048 * (q + 1)],
+                out=a_rows[:, 2048 * q : 2048 * (q + 1)],
                 in_=a[256 * q : 256 * (q + 1), :].rearrange("(p e) m -> p (e m)", e=2),
             )
 
-        x_words = x_sb[:].bitcast(F32).rearrange("b (q p e h) -> b q e h p", q=4, p=P, e=2, h=6)
-        a32 = a_sb[:].bitcast(F32)
+        def operand(name, columns):
+            grouped = keep.tile([P, SLOTS * columns], BF16, name=name + "_grouped", align_bytes=64)
+            codes = keep.tile([P, columns], U32, name=name + "_codes", align_bytes=64)
+            scales = keep.tile([P, columns], U8, name=name + "_scales", align_bytes=64)
+            return grouped, (codes, scales)
 
-        xg = keep.tile([P, 12288], BF16, name="xg", align_bytes=64)
-        xc = keep.tile([P, 3072], U32, name="xc", align_bytes=64)
-        xs = keep.tile([P, 3072], U8, name="xs", align_bytes=64)
-        alg = keep.tile([P, 8192], BF16, name="alg", align_bytes=64)
-        alc = keep.tile([P, 2048], U32, name="alc", align_bytes=64)
-        als = keep.tile([P, 2048], U8, name="als", align_bytes=64)
-        arg = keep.tile([P, 8192], BF16, name="arg", align_bytes=64)
-        arc = keep.tile([P, 2048], U32, name="arc", align_bytes=64)
-        ars = keep.tile([P, 2048], U8, name="ars", align_bytes=64)
-        t2g = keep.tile([P, 8192], BF16, name="t2g", align_bytes=64)
-        t2c = keep.tile([P, 2048], U32, name="t2c", align_bytes=64)
-        t2s = keep.tile([P, 2048], U8, name="t2s", align_bytes=64)
-        alg32 = alg[:].bitcast(F32)
+        x_grouped, x_mx = operand("x", PASSES * COLS)
+        left_grouped, left_mx = operand("left", PASSES * NODES)
+        right_grouped, right_mx = operand("right", PASSES * NODES)
+        t2_grouped, t2_mx = operand("t2", PASSES * NODES)
 
-        def quant(codes, scales, grouped, w0, w):
-            nc.vector.quantize_mx(
-                out=codes[:, w0 : w0 + w].bitcast(FP8X4),
-                scales=scales[:, w0 : w0 + w],
-                in_=grouped[:, 4 * w0 : 4 * (w0 + w)],
-            )
+        x_words = x_rows[:].bitcast(F32).rearrange("b (q p e h) -> b q e h p", q=4, p=P, e=2, h=STEP_PAIRS)
+        x_banks = {}
 
-        def mx(dst, lc, ls, l0, rc, rs, r0, n, start, stop):
-            nc.tensor.matmul_mx(
-                out=dst,
-                lhsT=lc[:, l0 : l0 + P].bitcast(FP8X4),
-                lhsT_scale=ls[:, l0 : l0 + P],
-                rhs=rc[:, r0 : r0 + n].bitcast(FP8X4),
-                rhs_scale=rs[:, r0 : r0 + n],
-                start=start,
-                stop=stop,
-            )
-
-        banks = {}
-
-        def xt(g, u):
-            for h in range(6):
+        def x_transposes(g, u):
+            for h in range(STEP_PAIRS):
                 if u == 0:
-                    banks[("x", g, h)] = psum.tile([P, 512], F32, name="bank", tag="bank")
+                    x_banks[(g, h)] = new_bank()
                 for e in range(2):
                     t = 2 * u + e
-                    nc.tensor.transpose(banks[("x", g, h)][:, t * P : (t + 1) * P], x_words[:, 2 * g + u, e, h, :], ident)
+                    nc.tensor.transpose(x_banks[(g, h)][:, t * P : (t + 1) * P], x_words[:, 2 * g + u, e, h, :], identity)
 
-        def xe(g, h, eng):
-            o = (g * 6 + h) * 1024
+        def x_regroup(g, h, engine):
+            first = SLOTS * (g * COLS + h * 2 * P)
             copy(
-                eng,
-                xg[:, o : o + 1024].rearrange("p (b k t) -> p b k t", k=2, t=4),
-                banks[("x", g, h)][:].bitcast(BF16).rearrange("p (t b k) -> p b k t", t=4, k=2),
+                engine,
+                x_grouped[:, first : first + SLOTS * 2 * P].rearrange("p (b k t) -> p b k t", k=2, t=SLOTS),
+                x_banks[(g, h)][:].bitcast(BF16).rearrange("p (t b k) -> p b k t", t=SLOTS, k=2),
             )
 
-        def at(tau, eng):
-            bank = psum.tile([P, 512], F32, name="bank", tag="bank")
+        def x_quantise(g, c):
+            quantise(x_mx[0], x_mx[1], x_grouped, g * COLS + c * CHUNK, CHUNK)
+
+        a_words = a_rows[:].bitcast(F32)
+        left_words = left_grouped[:].bitcast(F32)
+
+        def left_tile(tau):
+            bank = new_bank()
             for i in range(4):
-                nc.tensor.transpose(bank[:, i * P : (i + 1) * P], a32[:, tau * 512 + i * P : tau * 512 + (i + 1) * P], ident)
+                first = tau * ROW_WORDS + i * P
+                nc.tensor.transpose(bank[:, i * P : (i + 1) * P], a_words[:, first : first + P], identity)
             copy(
-                eng,
-                alg32[:, tau * 512 : (tau + 1) * 512].rearrange("p (g n u) -> p g n u", g=2, u=2),
-                bank[:].rearrange("p (g u n) -> p g n u", g=2, u=2),
+                "scalar",
+                left_words[:, tau * ROW_WORDS : (tau + 1) * ROW_WORDS].rearrange("p (g n u) -> p g n u", g=PASSES, u=2),
+                bank[:].rearrange("p (g u n) -> p g n u", g=PASSES, u=2),
             )
 
-        a_rows = a_sb[:].rearrange("p (g j q n e) -> p g q e n j", g=2, j=4, q=4, n=P, e=2)
+        def left_quantise(tau):
+            quantise(left_mx[0], left_mx[1], left_grouped, tau * PASSES * P, PASSES * P)
 
-        def ar(g, q):
-            o = g * 4096 + q * 1024
+        a_by_tile = a_rows[:].rearrange("p (g t q n e) -> p g q e n t", g=PASSES, t=SLOTS, q=4, n=P, e=2)
+
+        def right_regroup(g, q):
+            first = SLOTS * (g * NODES + q * 2 * P)
             nc.vector.tensor_copy(
-                out=arg[:, o : o + 1024].rearrange("p (e n j) -> p e n j", e=2, j=4),
-                in_=a_rows[:, g, q],
+                out=right_grouped[:, first : first + SLOTS * 2 * P].rearrange("p (e n t) -> p e n t", e=2, t=SLOTS),
+                in_=a_by_tile[:, g, q],
             )
 
-        res_tiles = {}
+        result_tiles = {}
 
-        def ypass(term, tau, c, lc, ls, eng):
-            bank = psum.tile([P, 512], F32, name="bank", tag="bank")
-            for g in range(2):
-                mx(bank[:], lc, ls, tau * 256 + g * P, xc, xs, g * 1536 + c * 512, 512, g == 0, g == 1)
+        def y_chunk(term, tau, c, left, engine):
+            bank = new_bank()
+            for g in range(PASSES):
+                mx_pass(bank[:], left, (tau * PASSES + g) * P, x_mx, g * COLS + c * CHUNK, CHUNK, g)
             if c == 0:
-                res = resp.tile([P, 1536], F32, name="res", tag="res")
-                res_tiles[(term, tau)] = res
-            res = res_tiles[(term, tau)]
+                result_tiles[(term, tau)] = results.tile([P, COLS], F32, name="result", tag="result")
+            result = result_tiles[(term, tau)]
             copy(
-                eng,
-                res[:].rearrange("p (b l) -> p b l", l=12)[:, :, 4 * c : 4 * c + 4].rearrange("p b (h k) -> p b h k", k=2),
+                engine,
+                result[:].rearrange("p (b l) -> p b l", l=12)[:, :, 4 * c : 4 * c + 4].rearrange("p b (h k) -> p b h k", k=2),
                 bank[:].rearrange("p (h b k) -> p b h k", h=2, k=2),
             )
-            if c == 2:
-                dst = out[:, term].rearrange("b (q p e) c l -> q e p b (c l)", q=4, p=P, e=2)[tau // 2, tau % 2]
-                nc.sync.dma_start(out=dst, in_=res[:].rearrange("p (b f) -> p b f", b=4))
+            if c == CHUNKS - 1:
+                rows = out[:, term].rearrange("b (q p e) c l -> q e p b (c l)", q=4, p=P, e=2)[tau // 2, tau % 2]
+                nc.sync.dma_start(out=rows, in_=result[:].rearrange("p (b f) -> p b f", b=4))
 
-        def ua(j):
-            for gp in range(2):
-                bank = psum.tile([P, 512], F32, name="bank", tag="bank")
-                for tp in range(4):
-                    for g in range(2):
-                        mx(bank[:, tp * P : (tp + 1) * P], arc, ars, g * 1024 + (4 * gp + tp) * P,
-                           alc, als, j * 256 + g * P, P, g == 0, g == 1)
-                o = j * 1024 + gp * 512
-                dst = t2g[:, o : o + 512].rearrange("p (n t) -> p n t", t=4)
-                src = bank[:].rearrange("p (t n) -> p n t", t=4)
-                if j // 4 == gp:
-                    w0 = (3 - j % 4) * P
+        def t2_tile(j):
+            for g2 in range(PASSES):
+                bank = new_bank()
+                for t in range(SLOTS):
+                    for g in range(PASSES):
+                        mx_pass(bank[:, t * P : (t + 1) * P], right_mx, g * NODES + (SLOTS * g2 + t) * P,
+                                left_mx, (j * PASSES + g) * P, P, g)
+                first = SLOTS * (j * PASSES + g2) * P
+                dst = t2_grouped[:, first : first + SLOTS * P].rearrange("p (n t) -> p n t", t=SLOTS)
+                src = bank[:].rearrange("p (t n) -> p n t", t=SLOTS)
+                if j // SLOTS == g2:
+                    window = (3 - j % SLOTS) * P
                     nc.vector.scalar_tensor_tensor(
                         out=dst, in0=src, scalar=2.0,
-                        in1=wide[:, w0 : w0 + 512].rearrange("p (t n) -> p n t", t=4),
+                        in1=eye_strip[:, window : window + SLOTS * P].rearrange("p (t n) -> p n t", t=SLOTS),
                         op0=ALU.mult, op1=ALU.subtract,
                     )
                 else:
                     nc.scalar.activation(out=dst, in_=src, func=ACT.Copy, scale=2.0)
+            quantise(t2_mx[0], t2_mx[1], t2_grouped, j * PASSES * P, PASSES * P)
 
-        def xq(g, c):
-            quant(xc, xs, xg, g * 1536 + c * 512, 512)
-
-        def aq(pair):
-            quant(alc, als, alg, pair * 512, 512)
-
-        xt(0, 0)
-        xt(0, 1)
-        for h in range(6):
-            xe(0, h, "v" if h % 2 == 0 else "s")
-        xt(1, 0)
-        xt(1, 1)
-        xe(1, 0, "s")
-        xe(1, 1, "v")
-        xq(0, 0)
-        at(0, "s")
-        at(1, "s")
-        xq(1, 0)
-        aq(0)
-        xe(1, 2, "s")
-        xe(1, 3, "v")
-        at(2, "s")
-        at(3, "s")
-        xq(0, 1)
-        aq(1)
-        xe(1, 4, "s")
-        xq(1, 1)
-        xe(1, 5, "v")
-        xq(0, 2)
-        xq(1, 2)
+        x_transposes(0, 0)
+        x_transposes(0, 1)
+        for h in range(STEP_PAIRS):
+            x_regroup(0, h, "vector" if h % 2 == 0 else "scalar")
+            if h == 3:
+                x_quantise(0, 0)
+        x_transposes(1, 0)
+        x_transposes(1, 1)
+        x_regroup(1, 0, "scalar")
+        x_regroup(1, 1, "vector")
         for tau in range(4):
-            ypass(0, tau, 0, alc, als, Y1_ENG[tau])
+            left_tile(tau)
+        x_quantise(1, 0)
+        left_quantise(0)
+        left_quantise(1)
+        x_regroup(1, 2, "scalar")
+        x_regroup(1, 3, "vector")
+        left_quantise(2)
+        left_quantise(3)
+        x_quantise(0, 1)
+        x_quantise(1, 1)
+        x_regroup(1, 4, "scalar")
+        x_regroup(1, 5, "vector")
+        x_quantise(0, 2)
+        x_quantise(1, 2)
+        for tau in range(4):
+            y_chunk(0, tau, 0, left_mx, "scalar")
         for q in range(4):
-            ar(0, q)
-        for tau in range(4, 8):
-            at(tau, "s")
-        aq(2)
-        aq(3)
-        for c in range(1, 3):
+            right_regroup(0, q)
+        for tau in range(4, TILES):
+            left_tile(tau)
+        for tau in range(4, TILES):
+            left_quantise(tau)
+        for c in range(1, CHUNKS):
             for tau in range(4):
-                ypass(0, tau, c, alc, als, Y1_ENG[tau])
+                y_chunk(0, tau, c, left_mx, "scalar")
         for q in range(4):
-            ar(1, q)
-        quant(arc, ars, arg, 0, 1024)
-        quant(arc, ars, arg, 1024, 1024)
-        for tau in range(4, 8):
-            for c in range(3):
-                ypass(0, tau, c, alc, als, Y1_ENG[tau])
-        for j in range(9):
-            if j < 8:
-                ua(j)
-                quant(t2c, t2s, t2g, j * 256, 256)
-            if j >= 1:
-                for c in range(3):
-                    ypass(1, j - 1, c, t2c, t2s, Y2_ENG[j - 1])
+            right_regroup(1, q)
+        for g in range(PASSES):
+            quantise(right_mx[0], right_mx[1], right_grouped, g * NODES, NODES)
+        for tau in range(4, TILES):
+            for c in range(CHUNKS):
+                y_chunk(0, tau, c, left_mx, "scalar" if tau < TILES - 1 else "vector")
+        for j in range(TILES + 1):
+            if j < TILES:
+                t2_tile(j)
+            if j > 0:
+                for c in range(CHUNKS):
+                    y_chunk(1, j - 1, c, t2_mx, "vector" if (j - 1) % 3 == 1 else "scalar")

@@ -175,6 +175,9 @@ def tile_gcn_pa_kernel(tc, a, x, out):
                     nc.scalar.activation(out=dst, in_=src, func=ACT.Copy, scale=2.0)
             quantise(t2_mx[0], t2_mx[1], t2_grouped, j * PASSES * P, PASSES * P)
 
+        def y1_engine(tau):
+            return "vector" if tau % 4 == 3 else "scalar"
+
         x_transposes(0, 0)
         x_transposes(0, 1)
         for h in range(STEP_PAIRS):
@@ -201,7 +204,7 @@ def tile_gcn_pa_kernel(tc, a, x, out):
         x_quantise(0, 2)
         x_quantise(1, 2)
         for tau in range(4):
-            y_chunk(0, tau, 0, left_mx, "scalar")
+            y_chunk(0, tau, 0, left_mx, y1_engine(tau))
         for q in range(4):
             right_regroup(0, q)
         for tau in range(4, TILES):
@@ -210,14 +213,14 @@ def tile_gcn_pa_kernel(tc, a, x, out):
             left_quantise(tau)
         for c in range(1, CHUNKS):
             for tau in range(4):
-                y_chunk(0, tau, c, left_mx, "scalar")
+                y_chunk(0, tau, c, left_mx, y1_engine(tau))
         for q in range(4):
             right_regroup(1, q)
         for g in range(PASSES):
             quantise(right_mx[0], right_mx[1], right_grouped, g * NODES, NODES)
         for tau in range(4, TILES):
             for c in range(CHUNKS):
-                y_chunk(0, tau, c, left_mx, "scalar" if tau < TILES - 1 else "vector")
+                y_chunk(0, tau, c, left_mx, y1_engine(tau))
         for j in range(TILES + 1):
             if j < TILES:
                 t2_tile(j)

@@ -27,7 +27,6 @@ FLOPS = 2 * NODES * NODES * (NODES + 2 * COLS)
 def tile_gcn_pa_kernel(tc, a, x, out):
     nc = tc.nc
     with ExitStack() as ctx:
-        ctx.enter_context(tc.manual_schedule())
         keep = ctx.enter_context(tc.tile_pool(name="keep", bufs=1))
         results = ctx.enter_context(tc.tile_pool(name="results", bufs=8))
         psum = ctx.enter_context(tc.psum_pool(name="psum", bufs=8))
@@ -175,9 +174,6 @@ def tile_gcn_pa_kernel(tc, a, x, out):
                     nc.scalar.activation(out=dst, in_=src, func=ACT.Copy, scale=2.0)
             quantise(t2_mx[0], t2_mx[1], t2_grouped, j * PASSES * P, PASSES * P)
 
-        def y1_engine(tau):
-            return "vector" if tau % 4 == 3 else "scalar"
-
         x_transposes(0, 0)
         x_transposes(0, 1)
         for h in range(STEP_PAIRS):
@@ -204,7 +200,7 @@ def tile_gcn_pa_kernel(tc, a, x, out):
         x_quantise(0, 2)
         x_quantise(1, 2)
         for tau in range(4):
-            y_chunk(0, tau, 0, left_mx, y1_engine(tau))
+            y_chunk(0, tau, 0, left_mx, "scalar")
         for q in range(4):
             right_regroup(0, q)
         for tau in range(4, TILES):
@@ -213,14 +209,14 @@ def tile_gcn_pa_kernel(tc, a, x, out):
             left_quantise(tau)
         for c in range(1, CHUNKS):
             for tau in range(4):
-                y_chunk(0, tau, c, left_mx, y1_engine(tau))
+                y_chunk(0, tau, c, left_mx, "scalar")
         for q in range(4):
             right_regroup(1, q)
         for g in range(PASSES):
             quantise(right_mx[0], right_mx[1], right_grouped, g * NODES, NODES)
         for tau in range(4, TILES):
             for c in range(CHUNKS):
-                y_chunk(0, tau, c, left_mx, y1_engine(tau))
+                y_chunk(0, tau, c, left_mx, "scalar" if tau < TILES - 1 else "vector")
         for j in range(TILES + 1):
             if j < TILES:
                 t2_tile(j)

from contextlib import ExitStack

import concourse.mybir as mybir
from concourse.masks import make_identity

F32 = mybir.dt.float32
BF16 = mybir.dt.bfloat16
U32 = mybir.dt.uint32
U8 = mybir.dt.uint8
FP8X4 = mybir.dt.float8_e4m3fn_x4
ALU = mybir.AluOpType
ACT = mybir.ActivationFunctionType

P = 128
TILES = 8
PASSES = 2
SLOTS = 4
NODES = 1024
STEP_PAIRS = 6
COLS = 1536
CHUNK = 512
CHUNKS = COLS // CHUNK
ROW_WORDS = NODES // 2
FLOPS = 2 * NODES * NODES * (NODES + 2 * COLS)


def tile_gcn_pa_kernel(tc, a, x, out):
    nc = tc.nc
    with ExitStack() as ctx:
        keep = ctx.enter_context(tc.tile_pool(name="keep", bufs=1))
        results = ctx.enter_context(tc.tile_pool(name="results", bufs=8))
        psum = ctx.enter_context(tc.psum_pool(name="psum", bufs=8))

        def new_bank():
            bank = psum.tile([P, CHUNK], F32, name="bank", tag="bank")
            return bank

        def copy(engine, dst, src):
            if engine == "vector":
                nc.vector.tensor_copy(out=dst, in_=src)
            else:
                nc.scalar.copy(out=dst, in_=src)

        def quantise(codes, scales, grouped, first, width):
            nc.vector.quantize_mx(
                out=codes[:, first : first + width].bitcast(FP8X4),
                scales=scales[:, first : first + width],
                in_=grouped[:, SLOTS * first : SLOTS * (first + width)],
            )

        def mx_pass(acc, left, left_first, right, right_first, width, g):
            nc.tensor.matmul_mx(
                out=acc,
                lhsT=left[0][:, left_first : left_first + P].bitcast(FP8X4),
                lhsT_scale=left[1][:, left_first : left_first + P],
                rhs=right[0][:, right_first : right_first + width].bitcast(FP8X4),
                rhs_scale=right[1][:, right_first : right_first + width],
                start=(g == 0),
                stop=(g == PASSES - 1),
            )

        eye_strip = keep.tile([P, 7 * P], F32, name="eye_strip")
        nc.gpsimd.memset(eye_strip[:], 0.0)
        make_identity(nc, eye_strip[:, 3 * P : 4 * P], nomemset=True)
        identity = eye_strip[:, 3 * P : 4 * P]

        x_rows = keep.tile([P, NODES * 12], BF16, name="x_rows")
        a_rows = keep.tile([P, TILES * NODES], BF16, name="a_rows")
        x_flat = x.rearrange("b c m l -> (b c) (m l)")
        for q in range(4):
            piece = slice(3072 * q, 3072 * (q + 1))
            nc.sync.dma_start(out=x_rows[:, piece], in_=x_flat[:, piece])
        for q in range(4):
            nc.sync.dma_start(
                out=a_rows[:, 2048 * q : 2048 * (q + 1)],
                in_=a[256 * q : 256 * (q + 1), :].rearrange("(p e) m -> p (e m)", e=2),
            )

        def operand(name, columns):
            grouped = keep.tile([P, SLOTS * columns], BF16, name=name + "_grouped", align_bytes=64)
            codes = keep.tile([P, columns], U32, name=name + "_codes", align_bytes=64)
            scales = keep.tile([P, columns], U8, name=name + "_scales", align_bytes=64)
            return grouped, (codes, scales)

        x_grouped, x_mx = operand("x", PASSES * COLS)
        left_grouped, left_mx = operand("left", PASSES * NODES)
        right_grouped, right_mx = operand("right", PASSES * NODES)
        t2_grouped, t2_mx = operand("t2", PASSES * NODES)

        x_words = x_rows[:].bitcast(F32).rearrange("b (q p e h) -> b q e h p", q=4, p=P, e=2, h=STEP_PAIRS)
        x_banks = {}

        def x_transposes(g, u):
            for h in range(STEP_PAIRS):
                if u == 0:
                    x_banks[(g, h)] = new_bank()
                for e in range(2):
                    t = 2 * u + e
                    nc.tensor.transpose(x_banks[(g, h)][:, t * P : (t + 1) * P], x_words[:, 2 * g + u, e, h, :], identity)

        def x_regroup(g, h, engine):
            first = SLOTS * (g * COLS + h * 2 * P)
            copy(
                engine,
                x_grouped[:, first : first + SLOTS * 2 * P].rearrange("p (b k t) -> p b k t", k=2, t=SLOTS),
                x_banks[(g, h)][:].bitcast(BF16).rearrange("p (t b k) -> p b k t", t=SLOTS, k=2),
            )

        def x_quantise(g, c):
            quantise(x_mx[0], x_mx[1], x_grouped, g * COLS + c * CHUNK, CHUNK)

        a_words = a_rows[:].bitcast(F32)
        left_words = left_grouped[:].bitcast(F32)

        def left_tile(tau):
            bank = new_bank()
            for i in range(4):
                first = tau * ROW_WORDS + i * P
                nc.tensor.transpose(bank[:, i * P : (i + 1) * P], a_words[:, first : first + P], identity)
            copy(
                "scalar",
                left_words[:, tau * ROW_WORDS : (tau + 1) * ROW_WORDS].rearrange("p (g n u) -> p g n u", g=PASSES, u=2),
                bank[:].rearrange("p (g u n) -> p g n u", g=PASSES, u=2),
            )

        def left_quantise(tau):
            quantise(left_mx[0], left_mx[1], left_grouped, tau * PASSES * P, PASSES * P)

        a_by_tile = a_rows[:].rearrange("p (g t q n e) -> p g q e n t", g=PASSES, t=SLOTS, q=4, n=P, e=2)

        def right_regroup(g, q):
            first = SLOTS * (g * NODES + q * 2 * P)
            nc.vector.tensor_copy(
                out=right_grouped[:, first : first + SLOTS * 2 * P].rearrange("p (e n t) -> p e n t", e=2, t=SLOTS),
                in_=a_by_tile[:, g, q],
            )

        result_tiles = {}

        def y_chunk(term, tau, c, left, engine):
            bank = new_bank()
            for g in range(PASSES):
                mx_pass(bank[:], left, (tau * PASSES + g) * P, x_mx, g * COLS + c * CHUNK, CHUNK, g)
            if c == 0:
                result_tiles[(term, tau)] = results.tile([P, COLS], F32, name="result", tag="result")
            result = result_tiles[(term, tau)]
            copy(
                engine,
                result[:].rearrange("p (b l) -> p b l", l=12)[:, :, 4 * c : 4 * c + 4].rearrange("p b (h k) -> p b h k", k=2),
                bank[:].rearrange("p (h b k) -> p b h k", h=2, k=2),
            )
            if c == CHUNKS - 1:
                rows = out[:, term].rearrange("b (q p e) c l -> q e p b (c l)", q=4, p=P, e=2)[tau // 2, tau % 2]
                nc.sync.dma_start(out=rows, in_=result[:].rearrange("p (b f) -> p b f", b=4))

        def t2_tile(j):
            for g2 in range(PASSES):
                bank = new_bank()
                for t in range(SLOTS):
                    for g in range(PASSES):
                        mx_pass(bank[:, t * P : (t + 1) * P], right_mx, g * NODES + (SLOTS * g2 + t) * P,
                                left_mx, (j * PASSES + g) * P, P, g)
                first = SLOTS * (j * PASSES + g2) * P
                dst = t2_grouped[:, first : first + SLOTS * P].rearrange("p (n t) -> p n t", t=SLOTS)
                src = bank[:].rearrange("p (t n) -> p n t", t=SLOTS)
                if j // SLOTS == g2:
                    window = (3 - j % SLOTS) * P
                    nc.vector.scalar_tensor_tensor(
                        out=dst, in0=src, scalar=2.0,
                        in1=eye_strip[:, window : window + SLOTS * P].rearrange("p (t n) -> p n t", t=SLOTS),
                        op0=ALU.mult, op1=ALU.subtract,
                    )
                else:
                    nc.scalar.activation(out=dst, in_=src, func=ACT.Copy, scale=2.0)
            quantise(t2_mx[0], t2_mx[1], t2_grouped, j * PASSES * P, PASSES * P)

        x_transposes(0, 0)
        x_transposes(0, 1)
        for h in range(STEP_PAIRS):
            x_regroup(0, h, "vector" if h % 2 == 0 else "scalar")
            if h == 3:
                x_quantise(0, 0)
        x_transposes(1, 0)
        x_transposes(1, 1)
        x_regroup(1, 0, "scalar")
        x_regroup(1, 1, "vector")
        for tau in range(4):
            left_tile(tau)
        x_quantise(1, 0)
        left_quantise(0)
        left_quantise(1)
        x_regroup(1, 2, "scalar")
        x_regroup(1, 3, "vector")
        left_quantise(2)
        left_quantise(3)
        x_quantise(0, 1)
        x_quantise(1, 1)
        x_regroup(1, 4, "scalar")
        x_regroup(1, 5, "vector")
        x_quantise(0, 2)
        x_quantise(1, 2)
        for tau in range(4):
            y_chunk(0, tau, 0, left_mx, "scalar")
        for q in range(4):
            right_regroup(0, q)
        for tau in range(4, TILES):
            left_tile(tau)
        for tau in range(4, TILES):
            left_quantise(tau)
        for c in range(1, CHUNKS):
            for tau in range(4):
                y_chunk(0, tau, c, left_mx, "scalar")
        for q in range(4):
            right_regroup(1, q)
        for g in range(PASSES):
            quantise(right_mx[0], right_mx[1], right_grouped, g * NODES, NODES)
        for tau in range(4, TILES):
            for c in range(CHUNKS):
                y_chunk(0, tau, c, left_mx, "scalar" if tau < TILES - 1 else "vector")
        for j in range(TILES + 1):
            if j < TILES:
                t2_tile(j)
            if j > 0:
                for c in range(CHUNKS):
                    y_chunk(1, j - 1, c, t2_mx, "vector" if (j - 1) % 3 == 1 else "scalar")
